import numpy as np
import ml_dtypes


def mxq(x, axis, fmt="e4m3"):
    dtype, down = {"e4m3": (ml_dtypes.float8_e4m3fn, 7), "e5m2": (ml_dtypes.float8_e5m2, 14)}[fmt]
    v = np.moveaxis(np.asarray(x, np.float32).astype(ml_dtypes.bfloat16).astype(np.float64), axis, -1)
    blocks = v.reshape(v.shape[:-1] + (-1, 32))
    amax = np.abs(blocks).max(-1, keepdims=True)
    byte = np.maximum(np.where(amax > 0, np.frexp(amax)[1] - 1 + 127, 0) - down, 1)
    scale = np.exp2(byte - 127.0)
    codes = (blocks / scale).astype(np.float32).astype(dtype).astype(np.float64)
    return np.moveaxis((codes * scale).reshape(v.shape), -1, axis)


WIDE = False


def mx_kscale(k):
    if not WIDE:
        return np.ones(k)
    levels = np.array([10, -10, 5, -5, 0])
    a = np.random.permutation(np.resize(levels, k // 512 * 4)).reshape(k // 512, 4)
    idx = np.arange(k)
    return np.exp2(a[idx // 512, idx % 128 // 32])


BF16 = ml_dtypes.bfloat16


def bf(x):
    return np.asarray(x, np.float32).astype(BF16)


def f64(x):
    return np.asarray(x).astype(np.float64)


E2M1 = np.array([0.0, 0.5, 1.0, 1.5, 2.0, 3.0, 4.0, 6.0, -0.0, -0.5, -1.0, -1.5, -2.0, -3.0, -4.0, -6.0])


def pack_weight(w, fmt):
    k, n = w.shape
    w = f64(bf(w)).reshape(k // 32, 32, n)
    amax = np.abs(w).max(1)
    if fmt == "e4m3":
        byte = np.frexp(amax)[1] - 1 + 127 - 7
    else:
        mant, ex = np.frexp(amax / 6.0)
        byte = np.where(mant > 0.5, ex, ex - 1) + 127
    byte = np.clip(np.where(amax > 0, byte, 1), 1, 254)
    scaled = (w * np.exp2(127.0 - byte)[:, None, :]).reshape(k, n).astype(np.float32)
    by_word = np.ascontiguousarray(scaled.reshape(k // 512, 128, 4, n).transpose(0, 1, 3, 2))
    if fmt == "e4m3":
        words = by_word.astype(ml_dtypes.float8_e4m3fn).view(np.uint8)
    else:
        c = by_word.astype(ml_dtypes.float4_e2m1fn).view(np.uint8) & 0xF
        words = c[..., 0::2] | (c[..., 1::2] << 4)
    return np.ascontiguousarray(words), np.ascontiguousarray(byte.astype(np.uint8).reshape(k // 512, 16, n))


def unpack_weight(words, scales, fmt):
    g, p, n, _ = words.shape
    if fmt == "e4m3":
        vals = np.ascontiguousarray(words).view(ml_dtypes.float8_e4m3fn).astype(np.float64)
    else:
        nib = np.empty((g, p, n, 4), np.uint8)
        nib[..., 0::2] = words & 0xF
        nib[..., 1::2] = words >> 4
        vals = E2M1[nib]
    vals = vals * np.repeat(np.exp2(scales.astype(np.float64) - 127.0), 8, axis=1)[..., None]
    return vals.transpose(0, 1, 3, 2).reshape(g * 512, n)


B, S, H, F = 4, 32, 2048, 4096


def setup_inputs():
    s, t = mx_kscale(H), mx_kscale(F)
    x = bf(np.random.standard_normal((B, S, H)) * s)
    Wg = np.random.standard_normal((H, F)) * 0.022 / s[:, None]
    Wu = np.random.standard_normal((H, F)) * 0.022 / s[:, None] * t
    Wd = np.random.standard_normal((F, H)) * 0.025 / t[:, None]
    gate_W_words, gate_W_scales = pack_weight(Wg, "e4m3")
    up_W_words, up_W_scales = pack_weight(Wu, "e4m3")
    down_W_words, down_W_scales = pack_weight(Wd, "e4m3")
    return {"x": x,
            "gate_W_words": gate_W_words, "gate_W_scales": gate_W_scales,
            "up_W_words": up_W_words, "up_W_scales": up_W_scales,
            "down_W_words": down_W_words, "down_W_scales": down_W_scales}


def reference(x, gate_W_words, gate_W_scales, up_W_words, up_W_scales, down_W_words, down_W_scales):
    b, s_len, h = x.shape
    xt = f64(x).reshape(b * s_len, h)
    Wg = unpack_weight(gate_W_words, gate_W_scales, "e4m3")
    Wu = unpack_weight(up_W_words, up_W_scales, "e4m3")
    Wd = unpack_weight(down_W_words, down_W_scales, "e4m3")
    xq = mxq(xt, 1, "e4m3")
    gate = xq @ Wg
    up = xq @ Wu
    gelu = np.tanh(0.7978845608028654 * (gate + 0.044715 * gate ** 3)) * gate * 0.5 + gate * 0.5
    inter = gelu * up
    out = mxq(inter, 1, "e4m3") @ Wd
    return out.reshape(b, s_len, h)

@@ -1,0 +1,261 @@
+from contextlib import ExitStack
+
+import concourse.mybir as mybir
+from concourse.masks import make_identity
+
+F32 = mybir.dt.float32
+BF16 = mybir.dt.bfloat16
+I32 = mybir.dt.int32
+U8 = mybir.dt.uint8
+FP8X4 = mybir.dt.float8_e4m3fn_x4
+ACT = mybir.ActivationFunctionType
+ALU = mybir.AluOpType
+
+P = 128
+H = 2048
+F = 4096
+K_PASS = 512
+N_TILE = 512
+HG = H // K_PASS
+FG = F // K_PASS
+FN = F // N_TILE
+HN = H // N_TILE
+
+FLOPS = 2 * P * (2 * H * F + F * H)
+
+
+def tile_w4a16tvmmlp_kernel(
+    tc,
+    x,
+    gate_W_words,
+    gate_W_scales,
+    up_W_words,
+    up_W_scales,
+    down_W_words,
+    down_W_scales,
+    out,
+):
+    nc = tc.nc
+    with ExitStack() as ctx:
+        ctx.enter_context(tc.manual_schedule())
+        keep = ctx.enter_context(tc.tile_pool(name="keep", bufs=1))
+        wpool = ctx.enter_context(tc.tile_pool(name="wpool", bufs=9))
+        psum = ctx.enter_context(tc.psum_pool(name="psum", bufs=1))
+
+        def bank(n, shape, dtype, name):
+            return psum.tile(shape, dtype, tag="bank%d" % n, name=name)
+
+        warm = keep.tile([P, 8], F32, name="warm")
+        gate_pl = keep.tile([P, F], U8, name="gate_pl", align_bytes=64)
+        up_pl = keep.tile([P, F], U8, name="up_pl", align_bytes=64)
+        down_pl = keep.tile([P, 2, H], U8, name="down_pl", align_bytes=64)
+        nc.vector.memset(warm[:], 0.0)
+        nc.vector.memset(gate_pl[:].bitcast(I32), 0)
+        nc.vector.memset(up_pl[:].bitcast(I32), 0)
+        nc.vector.memset(down_pl[:].bitcast(I32), 0)
+        nc.scalar.activation(out=warm[:], in_=warm[:], func=ACT.Gelu_apprx_tanh)
+
+        ident_f = keep.tile([P, P], F32, name="ident_f")
+        ident_b = keep.tile([P, P], BF16, name="ident_b")
+        make_identity(nc, ident_f[:])
+        make_identity(nc, ident_b[:])
+
+        x_sb = keep.tile([P, H], BF16, name="x_sb")
+        nc.sync.dma_start(out=x_sb[:], in_=x.rearrange("b s h -> (b s) h"))
+
+        for q in range(4):
+            nc.sync.dma_start(
+                out=gate_pl[32 * q : 32 * q + 16, :].bitcast(I32),
+                in_=gate_W_scales[:, 4 * q : 4 * q + 4, :].bitcast(I32),
+            )
+        for q in range(4):
+            nc.sync.dma_start(
+                out=up_pl[32 * q : 32 * q + 16, :].bitcast(I32),
+                in_=up_W_scales[:, 4 * q : 4 * q + 4, :].bitcast(I32),
+            )
+        for a in range(2):
+            for q in range(4):
+                nc.sync.dma_start(
+                    out=down_pl[32 * q : 32 * q + 16, a, :].bitcast(I32),
+                    in_=down_W_scales[4 * a : 4 * a + 4, 4 * q : 4 * q + 4, :].bitcast(I32),
+                )
+
+        def load_group(words, g, name):
+            t = wpool.tile([P, F], I32, tag="w", name=name, align_bytes=64)
+            nc.sync.dma_start(out=t[:], in_=words[g].rearrange("p n t -> p (n t)").bitcast(I32))
+            return t
+
+        def load_down_pair(a):
+            t = wpool.tile([P, 2, H], I32, tag="w", name="dw%d" % a, align_bytes=64)
+            nc.sync.dma_start(
+                out=t[:],
+                in_=down_W_words[2 * a : 2 * a + 2].rearrange("g p n t -> p g (n t)").bitcast(I32),
+            )
+            return t
+
+        gw = [load_group(gate_W_words, g, "gw%d" % g) for g in range(HG)]
+        uw = [load_group(up_W_words, g, "uw%d" % g) for g in range(HG)]
+        dpair = [load_down_pair(0)]
+
+        xw = x_sb[:].bitcast(F32)
+        xg = keep.tile([P, H], BF16, name="xg", align_bytes=64)
+        xgw = xg[:].bitcast(F32).rearrange("p (g r u) -> p g r u", g=HG, u=2)
+        xq = keep.tile([P, HG * P], I32, name="xq", align_bytes=64)
+        xpl = keep.tile([P, HG * P], U8, name="xpl", align_bytes=64)
+        for j in range(2):
+            xt = bank(j, [P, 4, P], F32, "xt%d" % j)
+            for i in range(4):
+                g, u = 2 * j + i // 2, i % 2
+                nc.tensor.transpose(xt[:, i, :], xw[:, 256 * g + u : 256 * (g + 1) : 2], ident_f[:])
+            src = xt[:].rearrange("p (g u) r -> p g r u", u=2)
+            if j == 0:
+                nc.vector.tensor_copy(out=xgw[:, 0:2], in_=src)
+            else:
+                nc.scalar.copy(out=xgw[:, 2:4], in_=src)
+        nc.vector.quantize_mx(out=xq[:].bitcast(FP8X4), scales=xpl[:], in_=xg[:])
+
+        def hidden_pass(acc, words, planes, g, n):
+            cols = slice(n * N_TILE, (n + 1) * N_TILE)
+            toks = slice(g * P, (g + 1) * P)
+            nc.tensor.matmul_mx(
+                out=acc[:],
+                lhsT=xq[:, toks].bitcast(FP8X4),
+                lhsT_scale=xpl[:, toks],
+                rhs=words[g][:, cols].bitcast(FP8X4),
+                rhs_scale=planes[4 * g : P, cols],
+                start=(g == 0),
+                stop=(g == HG - 1),
+            )
+
+        ga = [bank(n, [P, N_TILE], F32, "ga%d" % n) for n in range(FN)]
+        d6 = None
+        d7 = []
+        for g in range(HG):
+            for n in range(FN):
+                hidden_pass(ga[n], gw, gate_pl, g, n)
+            if g == 0:
+                dpair.append(load_down_pair(1))
+            if g == 1:
+                dpair.append(load_down_pair(2))
+                d6 = keep.tile([P, H], I32, name="d6", align_bytes=64)
+                nc.sync.dma_start(
+                    out=d6[:], in_=down_W_words[6].rearrange("p n t -> p (n t)").bitcast(I32)
+                )
+                last = down_W_words[7].rearrange("p n t -> p (n t)")
+                for c in range(HN):
+                    t = keep.tile([P, N_TILE], I32, name="d7_%d" % c, align_bytes=64)
+                    nc.sync.dma_start(
+                        out=t[:], in_=last[:, 4 * c * N_TILE : 4 * (c + 1) * N_TILE].bitcast(I32)
+                    )
+                    d7.append(t)
+
+        gelu_sb = keep.tile([P, FN, 4, P], F32, name="gelu_sb")
+        for n in range(FN):
+            nc.scalar.activation(
+                out=gelu_sb[:, n],
+                in_=ga[n][:].rearrange("p (c t) -> p t c", t=4),
+                func=ACT.Gelu_apprx_tanh,
+            )
+
+        ua = [bank(n, [P, N_TILE], F32, "ua%d" % n) for n in range(FN)]
+        for g in range(HG):
+            for n in range(FN):
+                hidden_pass(ua[n], uw, up_pl, g, n)
+
+        inter = [None] * FN
+        tps = [None] * FN
+        iq = [None] * FN
+        ipl = [None] * FN
+        grouped = [None] * FN
+
+        def mul(n):
+            inter[n] = keep.tile([P, 4, P], BF16, name="inter%d" % n)
+            nc.vector.tensor_tensor(
+                out=inter[n][:],
+                in0=ua[n][:].rearrange("p (c t) -> p t c", t=4),
+                in1=gelu_sb[:, n],
+                op=ALU.mult,
+            )
+
+        def flip(n):
+            tps[n] = bank(n, [P, 4, P], BF16, "tp%d" % n)
+            for t in range(4):
+                nc.tensor.transpose(tps[n][:, t, :], inter[n][:, t, :], ident_b[:])
+
+        def regroup(n):
+            grouped[n] = keep.tile([P, P, 4], BF16, name="grouped%d" % n, align_bytes=64)
+            nc.scalar.copy(out=grouped[n][:], in_=tps[n][:].rearrange("p t r -> p r t"))
+
+        def quantise(n):
+            iq[n] = keep.tile([P, P], I32, name="iq%d" % n, align_bytes=64)
+            ipl[n] = keep.tile([P, P], U8, name="ipl%d" % n, align_bytes=64)
+            nc.vector.quantize_mx(
+                out=iq[n][:].bitcast(FP8X4),
+                scales=ipl[n][:],
+                in_=grouped[n][:].rearrange("p r t -> p (r t)"),
+            )
+
+        oa = [None] * HN
+
+        def down_words(g, c):
+            cols = slice(c * N_TILE, (c + 1) * N_TILE)
+            if g < 6:
+                return dpair[g // 2][:, g % 2, cols]
+            if g == 6:
+                return d6[:, cols]
+            return d7[c][:]
+
+        def down_pass(g, c):
+            cols = slice(c * N_TILE, (c + 1) * N_TILE)
+            nc.tensor.matmul_mx(
+                out=oa[c][:],
+                lhsT=iq[g][:].bitcast(FP8X4),
+                lhsT_scale=ipl[g][:],
+                rhs=down_words(g, c).bitcast(FP8X4),
+                rhs_scale=down_pl[4 * (g % 4) : P, g // 4, cols],
+                start=(g == 0),
+                stop=(g == FG - 1),
+            )
+
+        for n in range(4):
+            mul(n)
+        for n in range(4):
+            flip(n)
+        for n in range(4):
+            regroup(n)
+        mul(4)
+        mul(5)
+        quantise(0)
+        quantise(1)
+        flip(4)
+        flip(5)
+        regroup(4)
+        regroup(5)
+        for c in range(HN):
+            oa[c] = bank(c, [P, N_TILE], F32, "oa%d" % c)
+        for g in range(2):
+            for c in range(HN):
+                down_pass(g, c)
+        mul(6)
+        mul(7)
+        quantise(2)
+        quantise(3)
+        flip(6)
+        flip(7)
+        regroup(6)
+        regroup(7)
+        for n in range(4, FN):
+            quantise(n)
+        for g in range(2, FG - 1):
+            for c in range(HN):
+                down_pass(g, c)
+
+        out2d = out.rearrange("b s h -> (b s) h")
+        for c in range(HN):
+            down_pass(FG - 1, c)
+            res = keep.tile([P, N_TILE], F32, name="res%d" % c)
+            if c % 2 == 0:
+                nc.vector.tensor_copy(out=res[:], in_=oa[c][:])
+            else:
+                nc.scalar.copy(out=res[:], in_=oa[c][:])
+            nc.sync.dma_start(out=out2d[:, c * N_TILE : (c + 1) * N_TILE], in_=res[:])

@@ -58,27 +58,27 @@ def tile_w4a16tvmmlp_kernel(
         ident_f = keep.tile([P, P], F32, name="ident_f")
         ident_b = keep.tile([P, P], BF16, name="ident_b")
         make_identity(nc, ident_f[:])
-        make_identity(nc, ident_b[:])
 
         x_sb = keep.tile([P, H], BF16, name="x_sb")
         nc.sync.dma_start(out=x_sb[:], in_=x.rearrange("b s h -> (b s) h"))
 
         for q in range(4):
-            nc.sync.dma_start(
-                out=gate_pl[32 * q : 32 * q + 16, :].bitcast(I32),
-                in_=gate_W_scales[:, 4 * q : 4 * q + 4, :].bitcast(I32),
+            nc.gpsimd.dma_start(
+                out=gate_pl[32 * q : 32 * q + 16, :].bitcast(F32),
+                in_=gate_W_scales[:, 4 * q : 4 * q + 4, :].bitcast(F32),
             )
         for q in range(4):
-            nc.sync.dma_start(
-                out=up_pl[32 * q : 32 * q + 16, :].bitcast(I32),
-                in_=up_W_scales[:, 4 * q : 4 * q + 4, :].bitcast(I32),
+            nc.gpsimd.dma_start(
+                out=up_pl[32 * q : 32 * q + 16, :].bitcast(F32),
+                in_=up_W_scales[:, 4 * q : 4 * q + 4, :].bitcast(F32),
             )
         for a in range(2):
             for q in range(4):
-                nc.sync.dma_start(
-                    out=down_pl[32 * q : 32 * q + 16, a, :].bitcast(I32),
-                    in_=down_W_scales[4 * a : 4 * a + 4, 4 * q : 4 * q + 4, :].bitcast(I32),
+                nc.gpsimd.dma_start(
+                    out=down_pl[32 * q : 32 * q + 16, a, :].bitcast(F32),
+                    in_=down_W_scales[4 * a : 4 * a + 4, 4 * q : 4 * q + 4, :].bitcast(F32),
                 )
+        make_identity(nc, ident_b[:])
 
         def load_group(words, g, name):
             t = wpool.tile([P, F], I32, tag="w", name=name, align_bytes=64)

@@ -49,10 +49,10 @@ def tile_w4a16tvmmlp_kernel(
         gate_pl = keep.tile([P, F], U8, name="gate_pl", align_bytes=64)
         up_pl = keep.tile([P, F], U8, name="up_pl", align_bytes=64)
         down_pl = keep.tile([P, 2, H], U8, name="down_pl", align_bytes=64)
-        nc.vector.memset(warm[:], 0.0)
         nc.vector.memset(gate_pl[:].bitcast(I32), 0)
-        nc.vector.memset(up_pl[:].bitcast(I32), 0)
         nc.vector.memset(down_pl[:].bitcast(I32), 0)
+        nc.vector.memset(up_pl[:].bitcast(I32), 0)
+        nc.vector.memset(warm[:], 0.0)
         nc.scalar.activation(out=warm[:], in_=warm[:], func=ACT.Gelu_apprx_tanh)
 
         ident_f = keep.tile([P, P], F32, name="ident_f")
@@ -62,23 +62,32 @@ def tile_w4a16tvmmlp_kernel(
         x_sb = keep.tile([P, H], BF16, name="x_sb")
         nc.sync.dma_start(out=x_sb[:], in_=x.rearrange("b s h -> (b s) h"))
 
-        for q in range(4):
-            nc.gpsimd.dma_start(
-                out=gate_pl[32 * q : 32 * q + 16, :].bitcast(F32),
-                in_=gate_W_scales[:, 4 * q : 4 * q + 4, :].bitcast(F32),
+        def hidden_scales(queue, view, planes, scales, q):
+            queue.dma_start(
+                out=planes[32 * q : 32 * q + 16, :].bitcast(view),
+                in_=scales[:, 4 * q : 4 * q + 4, :].bitcast(view),
             )
-        for q in range(4):
-            nc.gpsimd.dma_start(
-                out=up_pl[32 * q : 32 * q + 16, :].bitcast(F32),
-                in_=up_W_scales[:, 4 * q : 4 * q + 4, :].bitcast(F32),
+
+        def down_scales(a, q):
+            nc.sync.dma_start(
+                out=down_pl[32 * q : 32 * q + 16, a, :].bitcast(I32),
+                in_=down_W_scales[4 * a : 4 * a + 4, 4 * q : 4 * q + 4, :].bitcast(I32),
             )
-        for a in range(2):
-            for q in range(4):
-                nc.gpsimd.dma_start(
-                    out=down_pl[32 * q : 32 * q + 16, a, :].bitcast(F32),
-                    in_=down_W_scales[4 * a : 4 * a + 4, 4 * q : 4 * q + 4, :].bitcast(F32),
-                )
+
+        for planes, scales in ((gate_pl, gate_W_scales), (up_pl, up_W_scales)):
+            for q in (2, 3):
+                hidden_scales(nc.gpsimd, F32, planes, scales, q)
         make_identity(nc, ident_b[:])
+
+        for a in range(2):
+            for q in (0, 1):
+                down_scales(a, q)
+        for planes, scales in ((gate_pl, gate_W_scales), (up_pl, up_W_scales)):
+            for q in (0, 1):
+                hidden_scales(nc.sync, I32, planes, scales, q)
+        for a in range(2):
+            for q in (2, 3):
+                down_scales(a, q)
 
         def load_group(words, g, name):
             t = wpool.tile([P, F], I32, tag="w", name=name, align_bytes=64)

@@ -19,7 +19,7 @@ N_TILE = 512
 HG = H // K_PASS
 FG = F // K_PASS
 FN = F // N_TILE
-HN = H // N_TILE
+OUT_BLOCKS = ((0, 512), (512, 512), (1024, 512), (1536, 256), (1792, 256))
 
 FLOPS = 2 * P * (2 * H * F + F * H)
 
@@ -49,8 +49,8 @@ def tile_w4a16tvmmlp_kernel(
         gate_pl = keep.tile([P, F], U8, name="gate_pl", align_bytes=64)
         up_pl = keep.tile([P, F], U8, name="up_pl", align_bytes=64)
         down_pl = keep.tile([P, 2, H], U8, name="down_pl", align_bytes=64)
-        nc.vector.memset(gate_pl[:].bitcast(I32), 0)
         nc.vector.memset(down_pl[:].bitcast(I32), 0)
+        nc.vector.memset(gate_pl[:].bitcast(I32), 0)
         nc.vector.memset(up_pl[:].bitcast(I32), 0)
         nc.vector.memset(warm[:], 0.0)
         nc.scalar.activation(out=warm[:], in_=warm[:], func=ACT.Gelu_apprx_tanh)
@@ -58,14 +58,15 @@ def tile_w4a16tvmmlp_kernel(
         ident_f = keep.tile([P, P], F32, name="ident_f")
         ident_b = keep.tile([P, P], BF16, name="ident_b")
         make_identity(nc, ident_f[:])
+        make_identity(nc, ident_b[:])
 
         x_sb = keep.tile([P, H], BF16, name="x_sb")
         nc.sync.dma_start(out=x_sb[:], in_=x.rearrange("b s h -> (b s) h"))
 
-        def hidden_scales(queue, view, planes, scales, q):
-            queue.dma_start(
-                out=planes[32 * q : 32 * q + 16, :].bitcast(view),
-                in_=scales[:, 4 * q : 4 * q + 4, :].bitcast(view),
+        def hidden_scales(planes, scales, q):
+            nc.sync.dma_start(
+                out=planes[32 * q : 32 * q + 16, :].bitcast(I32),
+                in_=scales[:, 4 * q : 4 * q + 4, :].bitcast(I32),
             )
 
         def down_scales(a, q):
@@ -74,20 +75,13 @@ def tile_w4a16tvmmlp_kernel(
                 in_=down_W_scales[4 * a : 4 * a + 4, 4 * q : 4 * q + 4, :].bitcast(I32),
             )
 
-        for planes, scales in ((gate_pl, gate_W_scales), (up_pl, up_W_scales)):
-            for q in (2, 3):
-                hidden_scales(nc.gpsimd, F32, planes, scales, q)
-        make_identity(nc, ident_b[:])
-
-        for a in range(2):
-            for q in (0, 1):
-                down_scales(a, q)
-        for planes, scales in ((gate_pl, gate_W_scales), (up_pl, up_W_scales)):
-            for q in (0, 1):
-                hidden_scales(nc.sync, I32, planes, scales, q)
-        for a in range(2):
-            for q in (2, 3):
-                down_scales(a, q)
+        for quads in ((2, 3), (0, 1)):
+            for a in range(2):
+                for q in quads:
+                    down_scales(a, q)
+            for planes, scales in ((gate_pl, gate_W_scales), (up_pl, up_W_scales)):
+                for q in quads:
+                    hidden_scales(planes, scales, q)
 
         def load_group(words, g, name):
             t = wpool.tile([P, F], I32, tag="w", name=name, align_bytes=64)
@@ -96,10 +90,11 @@ def tile_w4a16tvmmlp_kernel(
 
         def load_down_pair(a):
             t = wpool.tile([P, 2, H], I32, tag="w", name="dw%d" % a, align_bytes=64)
-            nc.sync.dma_start(
-                out=t[:],
-                in_=down_W_words[2 * a : 2 * a + 2].rearrange("g p n t -> p g (n t)").bitcast(I32),
-            )
+            for i in range(2):
+                nc.sync.dma_start(
+                    out=t[:, i, :],
+                    in_=down_W_words[2 * a + i].rearrange("p n t -> p (n t)").bitcast(I32),
+                )
             return t
 
         gw = [load_group(gate_W_words, g, "gw%d" % g) for g in range(HG)]
@@ -151,11 +146,9 @@ def tile_w4a16tvmmlp_kernel(
                     out=d6[:], in_=down_W_words[6].rearrange("p n t -> p (n t)").bitcast(I32)
                 )
                 last = down_W_words[7].rearrange("p n t -> p (n t)")
-                for c in range(HN):
-                    t = keep.tile([P, N_TILE], I32, name="d7_%d" % c, align_bytes=64)
-                    nc.sync.dma_start(
-                        out=t[:], in_=last[:, 4 * c * N_TILE : 4 * (c + 1) * N_TILE].bitcast(I32)
-                    )
+                for c, (c0, cw) in enumerate(OUT_BLOCKS):
+                    t = keep.tile([P, cw], I32, name="d7_%d" % c, align_bytes=64)
+                    nc.sync.dma_start(out=t[:], in_=last[:, 4 * c0 : 4 * (c0 + cw)].bitcast(I32))
                     d7.append(t)
 
         gelu_sb = keep.tile([P, FN, 4, P], F32, name="gelu_sb")
@@ -204,10 +197,10 @@ def tile_w4a16tvmmlp_kernel(
                 in_=grouped[n][:].rearrange("p r t -> p (r t)"),
             )
 
-        oa = [None] * HN
+        oa = [None] * len(OUT_BLOCKS)
 
         def down_words(g, c):
-            cols = slice(c * N_TILE, (c + 1) * N_TILE)
+            cols = slice(OUT_BLOCKS[c][0], OUT_BLOCKS[c][0] + OUT_BLOCKS[c][1])
             if g < 6:
                 return dpair[g // 2][:, g % 2, cols]
             if g == 6:
@@ -215,7 +208,7 @@ def tile_w4a16tvmmlp_kernel(
             return d7[c][:]
 
         def down_pass(g, c):
-            cols = slice(c * N_TILE, (c + 1) * N_TILE)
+            cols = slice(OUT_BLOCKS[c][0], OUT_BLOCKS[c][0] + OUT_BLOCKS[c][1])
             nc.tensor.matmul_mx(
                 out=oa[c][:],
                 lhsT=iq[g][:].bitcast(FP8X4),
@@ -240,10 +233,10 @@ def tile_w4a16tvmmlp_kernel(
         flip(5)
         regroup(4)
         regroup(5)
-        for c in range(HN):
-            oa[c] = bank(c, [P, N_TILE], F32, "oa%d" % c)
+        for c, (c0, cw) in enumerate(OUT_BLOCKS):
+            oa[c] = bank(c, [P, cw], F32, "oa%d" % c)
         for g in range(2):
-            for c in range(HN):
+            for c in range(len(OUT_BLOCKS)):
                 down_pass(g, c)
         mul(6)
         mul(7)
@@ -256,15 +249,15 @@ def tile_w4a16tvmmlp_kernel(
         for n in range(4, FN):
             quantise(n)
         for g in range(2, FG - 1):
-            for c in range(HN):
+            for c in range(len(OUT_BLOCKS)):
                 down_pass(g, c)
 
         out2d = out.rearrange("b s h -> (b s) h")
-        for c in range(HN):
+        for c, (c0, cw) in enumerate(OUT_BLOCKS):
             down_pass(FG - 1, c)
-            res = keep.tile([P, N_TILE], F32, name="res%d" % c)
+            res = keep.tile([P, cw], F32, name="res%d" % c)
             if c % 2 == 0:
                 nc.vector.tensor_copy(out=res[:], in_=oa[c][:])
             else:
                 nc.scalar.copy(out=res[:], in_=oa[c][:])
-            nc.sync.dma_start(out=out2d[:, c * N_TILE : (c + 1) * N_TILE], in_=res[:])
+            nc.sync.dma_start(out=out2d[:, c0 : c0 + cw], in_=res[:])

@@ -49,24 +49,19 @@ def tile_w4a16tvmmlp_kernel(
         gate_pl = keep.tile([P, F], U8, name="gate_pl", align_bytes=64)
         up_pl = keep.tile([P, F], U8, name="up_pl", align_bytes=64)
         down_pl = keep.tile([P, 2, H], U8, name="down_pl", align_bytes=64)
-        nc.vector.memset(down_pl[:].bitcast(I32), 0)
         nc.vector.memset(gate_pl[:].bitcast(I32), 0)
         nc.vector.memset(up_pl[:].bitcast(I32), 0)
+        nc.vector.memset(down_pl[:].bitcast(I32), 0)
         nc.vector.memset(warm[:], 0.0)
         nc.scalar.activation(out=warm[:], in_=warm[:], func=ACT.Gelu_apprx_tanh)
-
-        ident_f = keep.tile([P, P], F32, name="ident_f")
-        ident_b = keep.tile([P, P], BF16, name="ident_b")
-        make_identity(nc, ident_f[:])
-        make_identity(nc, ident_b[:])
 
         x_sb = keep.tile([P, H], BF16, name="x_sb")
         nc.sync.dma_start(out=x_sb[:], in_=x.rearrange("b s h -> (b s) h"))
 
-        def hidden_scales(planes, scales, q):
-            nc.sync.dma_start(
-                out=planes[32 * q : 32 * q + 16, :].bitcast(I32),
-                in_=scales[:, 4 * q : 4 * q + 4, :].bitcast(I32),
+        def hidden_scales(queue, view, planes, scales, q):
+            queue.dma_start(
+                out=planes[32 * q : 32 * q + 16, :].bitcast(view),
+                in_=scales[:, 4 * q : 4 * q + 4, :].bitcast(view),
             )
 
         def down_scales(a, q):
@@ -75,13 +70,21 @@ def tile_w4a16tvmmlp_kernel(
                 in_=down_W_scales[4 * a : 4 * a + 4, 4 * q : 4 * q + 4, :].bitcast(I32),
             )
 
-        for quads in ((2, 3), (0, 1)):
+        for planes, scales in ((gate_pl, gate_W_scales), (up_pl, up_W_scales)):
+            for q in (2, 3):
+                hidden_scales(nc.gpsimd, F32, planes, scales, q)
+        ident_f = keep.tile([P, P], F32, name="ident_f")
+        ident_b = keep.tile([P, P], BF16, name="ident_b")
+        make_identity(nc, ident_f[:])
+        make_identity(nc, ident_b[:])
+
+        for planes, scales in ((gate_pl, gate_W_scales), (up_pl, up_W_scales)):
+            for q in (0, 1):
+                hidden_scales(nc.sync, I32, planes, scales, q)
+        for quads in ((0, 1), (2, 3)):
             for a in range(2):
                 for q in quads:
                     down_scales(a, q)
-            for planes, scales in ((gate_pl, gate_W_scales), (up_pl, up_W_scales)):
-                for q in quads:
-                    hidden_scales(planes, scales, q)
 
         def load_group(words, g, name):
             t = wpool.tile([P, F], I32, tag="w", name=name, align_bytes=64)

@@ -49,19 +49,24 @@ def tile_w4a16tvmmlp_kernel(
         gate_pl = keep.tile([P, F], U8, name="gate_pl", align_bytes=64)
         up_pl = keep.tile([P, F], U8, name="up_pl", align_bytes=64)
         down_pl = keep.tile([P, 2, H], U8, name="down_pl", align_bytes=64)
+        nc.vector.memset(down_pl[:].bitcast(I32), 0)
         nc.vector.memset(gate_pl[:].bitcast(I32), 0)
         nc.vector.memset(up_pl[:].bitcast(I32), 0)
-        nc.vector.memset(down_pl[:].bitcast(I32), 0)
         nc.vector.memset(warm[:], 0.0)
         nc.scalar.activation(out=warm[:], in_=warm[:], func=ACT.Gelu_apprx_tanh)
+
+        ident_f = keep.tile([P, P], F32, name="ident_f")
+        ident_b = keep.tile([P, P], BF16, name="ident_b")
+        make_identity(nc, ident_f[:])
+        make_identity(nc, ident_b[:])
 
         x_sb = keep.tile([P, H], BF16, name="x_sb")
         nc.sync.dma_start(out=x_sb[:], in_=x.rearrange("b s h -> (b s) h"))
 
-        def hidden_scales(queue, view, planes, scales, q):
-            queue.dma_start(
-                out=planes[32 * q : 32 * q + 16, :].bitcast(view),
-                in_=scales[:, 4 * q : 4 * q + 4, :].bitcast(view),
+        def hidden_scales(planes, scales, q):
+            nc.sync.dma_start(
+                out=planes[32 * q : 32 * q + 16, :].bitcast(I32),
+                in_=scales[:, 4 * q : 4 * q + 4, :].bitcast(I32),
             )
 
         def down_scales(a, q):
@@ -70,21 +75,13 @@ def tile_w4a16tvmmlp_kernel(
                 in_=down_W_scales[4 * a : 4 * a + 4, 4 * q : 4 * q + 4, :].bitcast(I32),
             )
 
-        for planes, scales in ((gate_pl, gate_W_scales), (up_pl, up_W_scales)):
-            for q in (2, 3):
-                hidden_scales(nc.gpsimd, F32, planes, scales, q)
-        ident_f = keep.tile([P, P], F32, name="ident_f")
-        ident_b = keep.tile([P, P], BF16, name="ident_b")
-        make_identity(nc, ident_f[:])
-        make_identity(nc, ident_b[:])
-
-        for planes, scales in ((gate_pl, gate_W_scales), (up_pl, up_W_scales)):
-            for q in (0, 1):
-                hidden_scales(nc.sync, I32, planes, scales, q)
-        for quads in ((0, 1), (2, 3)):
+        for quads in ((2, 3), (0, 1)):
             for a in range(2):
                 for q in quads:
                     down_scales(a, q)
+            for planes, scales in ((gate_pl, gate_W_scales), (up_pl, up_W_scales)):
+                for q in quads:
+                    hidden_scales(planes, scales, q)
 
         def load_group(words, g, name):
             t = wpool.tile([P, F], I32, tag="w", name=name, align_bytes=64)
@@ -102,7 +99,8 @@ def tile_w4a16tvmmlp_kernel(
 
         gw = [load_group(gate_W_words, g, "gw%d" % g) for g in range(HG)]
         uw = [load_group(up_W_words, g, "uw%d" % g) for g in range(HG)]
-        dpair = [load_down_pair(0)]
+        load_group(gate_W_words, 0, "extra")
+        dpair = []
 
         xw = x_sb[:].bitcast(F32)
         xg = keep.tile([P, H], BF16, name="xg", align_bytes=64)
@@ -140,10 +138,9 @@ def tile_w4a16tvmmlp_kernel(
         for g in range(HG):
             for n in range(FN):
                 hidden_pass(ga[n], gw, gate_pl, g, n)
-            if g == 0:
-                dpair.append(load_down_pair(1))
-            if g == 1:
-                dpair.append(load_down_pair(2))
+            if g < 3:
+                dpair.append(load_down_pair(g))
+            if g == 2:
                 d6 = keep.tile([P, H], I32, name="d6", align_bytes=64)
                 nc.sync.dma_start(
                     out=d6[:], in_=down_W_words[6].rearrange("p n t -> p (n t)").bitcast(I32)

from contextlib import ExitStack

import concourse.mybir as mybir
from concourse.masks import make_identity

F32 = mybir.dt.float32
BF16 = mybir.dt.bfloat16
I32 = mybir.dt.int32
U8 = mybir.dt.uint8
FP8X4 = mybir.dt.float8_e4m3fn_x4
ACT = mybir.ActivationFunctionType
ALU = mybir.AluOpType

P = 128
H = 2048
F = 4096
K_PASS = 512
N_TILE = 512
HG = H // K_PASS
FG = F // K_PASS
FN = F // N_TILE
OUT_BLOCKS = ((0, 512), (512, 512), (1024, 512), (1536, 256), (1792, 256))

FLOPS = 2 * P * (2 * H * F + F * H)


def tile_w4a16tvmmlp_kernel(
    tc,
    x,
    gate_W_words,
    gate_W_scales,
    up_W_words,
    up_W_scales,
    down_W_words,
    down_W_scales,
    out,
):
    nc = tc.nc
    with ExitStack() as ctx:
        ctx.enter_context(tc.manual_schedule())
        keep = ctx.enter_context(tc.tile_pool(name="keep", bufs=1))
        wpool = ctx.enter_context(tc.tile_pool(name="wpool", bufs=9))
        psum = ctx.enter_context(tc.psum_pool(name="psum", bufs=1))

        def bank(n, shape, dtype, name):
            return psum.tile(shape, dtype, tag="bank%d" % n, name=name)

        warm = keep.tile([P, 8], F32, name="warm")
        gate_pl = keep.tile([P, F], U8, name="gate_pl", align_bytes=64)
        up_pl = keep.tile([P, F], U8, name="up_pl", align_bytes=64)
        down_pl = keep.tile([P, 2, H], U8, name="down_pl", align_bytes=64)
        nc.vector.memset(down_pl[:].bitcast(I32), 0)
        nc.vector.memset(gate_pl[:].bitcast(I32), 0)
        nc.vector.memset(up_pl[:].bitcast(I32), 0)
        nc.vector.memset(warm[:], 0.0)
        nc.scalar.activation(out=warm[:], in_=warm[:], func=ACT.Gelu_apprx_tanh)

        ident_f = keep.tile([P, P], F32, name="ident_f")
        ident_b = keep.tile([P, P], BF16, name="ident_b")
        make_identity(nc, ident_f[:])
        make_identity(nc, ident_b[:])

        x_sb = keep.tile([P, H], BF16, name="x_sb")
        nc.sync.dma_start(out=x_sb[:], in_=x.rearrange("b s h -> (b s) h"))

        def hidden_scales(planes, scales, q):
            nc.sync.dma_start(
                out=planes[32 * q : 32 * q + 16, :].bitcast(I32),
                in_=scales[:, 4 * q : 4 * q + 4, :].bitcast(I32),
            )

        def down_scales(a, q):
            nc.sync.dma_start(
                out=down_pl[32 * q : 32 * q + 16, a, :].bitcast(I32),
                in_=down_W_scales[4 * a : 4 * a + 4, 4 * q : 4 * q + 4, :].bitcast(I32),
            )

        for quads in ((2, 3), (0, 1)):
            for a in range(2):
                for q in quads:
                    down_scales(a, q)
            for planes, scales in ((gate_pl, gate_W_scales), (up_pl, up_W_scales)):
                for q in quads:
                    hidden_scales(planes, scales, q)

        def load_group(words, g, name):
            t = wpool.tile([P, F], I32, tag="w", name=name, align_bytes=64)
            nc.sync.dma_start(out=t[:], in_=words[g].rearrange("p n t -> p (n t)").bitcast(I32))
            return t

        def load_down_pair(a):
            t = wpool.tile([P, 2, H], I32, tag="w", name="dw%d" % a, align_bytes=64)
            for i in range(2):
                nc.sync.dma_start(
                    out=t[:, i, :],
                    in_=down_W_words[2 * a + i].rearrange("p n t -> p (n t)").bitcast(I32),
                )
            return t

        gw = [load_group(gate_W_words, g, "gw%d" % g) for g in range(HG)]
        uw = [load_group(up_W_words, g, "uw%d" % g) for g in range(HG)]
        load_group(gate_W_words, 0, "extra")
        dpair = []

        xw = x_sb[:].bitcast(F32)
        xg = keep.tile([P, H], BF16, name="xg", align_bytes=64)
        xgw = xg[:].bitcast(F32).rearrange("p (g r u) -> p g r u", g=HG, u=2)
        xq = keep.tile([P, HG * P], I32, name="xq", align_bytes=64)
        xpl = keep.tile([P, HG * P], U8, name="xpl", align_bytes=64)
        for j in range(2):
            xt = bank(j, [P, 4, P], F32, "xt%d" % j)
            for i in range(4):
                g, u = 2 * j + i // 2, i % 2
                nc.tensor.transpose(xt[:, i, :], xw[:, 256 * g + u : 256 * (g + 1) : 2], ident_f[:])
            src = xt[:].rearrange("p (g u) r -> p g r u", u=2)
            if j == 0:
                nc.vector.tensor_copy(out=xgw[:, 0:2], in_=src)
            else:
                nc.scalar.copy(out=xgw[:, 2:4], in_=src)
        nc.vector.quantize_mx(out=xq[:].bitcast(FP8X4), scales=xpl[:], in_=xg[:])

        def hidden_pass(acc, words, planes, g, n):
            cols = slice(n * N_TILE, (n + 1) * N_TILE)
            toks = slice(g * P, (g + 1) * P)
            nc.tensor.matmul_mx(
                out=acc[:],
                lhsT=xq[:, toks].bitcast(FP8X4),
                lhsT_scale=xpl[:, toks],
                rhs=words[g][:, cols].bitcast(FP8X4),
                rhs_scale=planes[4 * g : P, cols],
                start=(g == 0),
                stop=(g == HG - 1),
            )

        ga = [bank(n, [P, N_TILE], F32, "ga%d" % n) for n in range(FN)]
        d6 = None
        d7 = []
        for g in range(HG):
            for n in range(FN):
                hidden_pass(ga[n], gw, gate_pl, g, n)
            if g < 3:
                dpair.append(load_down_pair(g))
            if g == 2:
                d6 = keep.tile([P, H], I32, name="d6", align_bytes=64)
                nc.sync.dma_start(
                    out=d6[:], in_=down_W_words[6].rearrange("p n t -> p (n t)").bitcast(I32)
                )
                last = down_W_words[7].rearrange("p n t -> p (n t)")
                for c, (c0, cw) in enumerate(OUT_BLOCKS):
                    t = keep.tile([P, cw], I32, name="d7_%d" % c, align_bytes=64)
                    nc.sync.dma_start(out=t[:], in_=last[:, 4 * c0 : 4 * (c0 + cw)].bitcast(I32))
                    d7.append(t)

        gelu_sb = keep.tile([P, FN, 4, P], F32, name="gelu_sb")
        for n in range(FN):
            nc.scalar.activation(
                out=gelu_sb[:, n],
                in_=ga[n][:].rearrange("p (c t) -> p t c", t=4),
                func=ACT.Gelu_apprx_tanh,
            )

        ua = [bank(n, [P, N_TILE], F32, "ua%d" % n) for n in range(FN)]
        for g in range(HG):
            for n in range(FN):
                hidden_pass(ua[n], uw, up_pl, g, n)

        inter = [None] * FN
        tps = [None] * FN
        iq = [None] * FN
        ipl = [None] * FN
        grouped = [None] * FN

        def mul(n):
            inter[n] = keep.tile([P, 4, P], BF16, name="inter%d" % n)
            nc.vector.tensor_tensor(
                out=inter[n][:],
                in0=ua[n][:].rearrange("p (c t) -> p t c", t=4),
                in1=gelu_sb[:, n],
                op=ALU.mult,
            )

        def flip(n):
            tps[n] = bank(n, [P, 4, P], BF16, "tp%d" % n)
            for t in range(4):
                nc.tensor.transpose(tps[n][:, t, :], inter[n][:, t, :], ident_b[:])

        def regroup(n):
            grouped[n] = keep.tile([P, P, 4], BF16, name="grouped%d" % n, align_bytes=64)
            nc.scalar.copy(out=grouped[n][:], in_=tps[n][:].rearrange("p t r -> p r t"))

        def quantise(n):
            iq[n] = keep.tile([P, P], I32, name="iq%d" % n, align_bytes=64)
            ipl[n] = keep.tile([P, P], U8, name="ipl%d" % n, align_bytes=64)
            nc.vector.quantize_mx(
                out=iq[n][:].bitcast(FP8X4),
                scales=ipl[n][:],
                in_=grouped[n][:].rearrange("p r t -> p (r t)"),
            )

        oa = [None] * len(OUT_BLOCKS)

        def down_words(g, c):
            cols = slice(OUT_BLOCKS[c][0], OUT_BLOCKS[c][0] + OUT_BLOCKS[c][1])
            if g < 6:
                return dpair[g // 2][:, g % 2, cols]
            if g == 6:
                return d6[:, cols]
            return d7[c][:]

        def down_pass(g, c):
            cols = slice(OUT_BLOCKS[c][0], OUT_BLOCKS[c][0] + OUT_BLOCKS[c][1])
            nc.tensor.matmul_mx(
                out=oa[c][:],
                lhsT=iq[g][:].bitcast(FP8X4),
                lhsT_scale=ipl[g][:],
                rhs=down_words(g, c).bitcast(FP8X4),
                rhs_scale=down_pl[4 * (g % 4) : P, g // 4, cols],
                start=(g == 0),
                stop=(g == FG - 1),
            )

        for n in range(4):
            mul(n)
        for n in range(4):
            flip(n)
        for n in range(4):
            regroup(n)
        mul(4)
        mul(5)
        quantise(0)
        quantise(1)
        flip(4)
        flip(5)
        regroup(4)
        regroup(5)
        for c, (c0, cw) in enumerate(OUT_BLOCKS):
            oa[c] = bank(c, [P, cw], F32, "oa%d" % c)
        for g in range(2):
            for c in range(len(OUT_BLOCKS)):
                down_pass(g, c)
        mul(6)
        mul(7)
        quantise(2)
        quantise(3)
        flip(6)
        flip(7)
        regroup(6)
        regroup(7)
        for n in range(4, FN):
            quantise(n)
        for g in range(2, FG - 1):
            for c in range(len(OUT_BLOCKS)):
                down_pass(g, c)

        out2d = out.rearrange("b s h -> (b s) h")
        for c, (c0, cw) in enumerate(OUT_BLOCKS):
            down_pass(FG - 1, c)
            res = keep.tile([P, cw], F32, name="res%d" % c)
            if c % 2 == 0:
                nc.vector.tensor_copy(out=res[:], in_=oa[c][:])
            else:
                nc.scalar.copy(out=res[:], in_=oa[c][:])
            nc.sync.dma_start(out=out2d[:, c0 : c0 + cw], in_=res[:])
